import numpy as np
import ml_dtypes


def mxq(x, axis, fmt="e4m3"):
    dtype, down = {"e4m3": (ml_dtypes.float8_e4m3fn, 7), "e5m2": (ml_dtypes.float8_e5m2, 14)}[fmt]
    v = np.moveaxis(np.asarray(x, np.float32).astype(ml_dtypes.bfloat16).astype(np.float64), axis, -1)
    blocks = v.reshape(v.shape[:-1] + (-1, 32))
    amax = np.abs(blocks).max(-1, keepdims=True)
    byte = np.maximum(np.where(amax > 0, np.frexp(amax)[1] - 1 + 127, 0) - down, 1)
    scale = np.exp2(byte - 127.0)
    codes = (blocks / scale).astype(np.float32).astype(dtype).astype(np.float64)
    return np.moveaxis((codes * scale).reshape(v.shape), -1, axis)


WIDE = False


def mx_kscale(k):
    if not WIDE:
        return np.ones(k)
    levels = np.array([10, -10, 5, -5, 0])
    a = np.random.permutation(np.resize(levels, k // 512 * 4)).reshape(k // 512, 4)
    idx = np.arange(k)
    return np.exp2(a[idx // 512, idx % 128 // 32])


BF16 = ml_dtypes.bfloat16


def bf(x):
    return np.asarray(x, np.float32).astype(BF16)


def f64(x):
    return np.asarray(x).astype(np.float64)


B, SD, A, H, HS, M, C, F1, F2 = 1024, 896, 128, 1024, 32, 896, 2, 2048, 300
K1 = SD + A
EPS = 1e-12


def l2norm(v):
    n = np.sqrt(np.sum(v * v, axis=-1, keepdims=True))
    return v / np.maximum(n, EPS)


def setup_inputs():
    s = mx_kscale(K1)
    g = np.where(np.arange(H) < HS, 1.0, 0.125)
    return {"state": bf(np.random.standard_normal((B, SD)) * s[:SD]),
            "action": bf(np.random.standard_normal((B, A)) * s[SD:]),
            "up_w1": bf(np.random.standard_normal((H, K1)) * g[:, None] / np.sqrt(K1) / s[None, :]),
            "up_b1": bf(np.random.standard_normal(H) * 0.5 * g),
            "up_w2_self": bf(np.random.standard_normal((H, H))),
            "up_b2": bf(np.random.standard_normal(H) * 0.3)}


def reference(state, action, up_w1, up_b1, up_w2_self, up_b2):
    xu = np.concatenate([f64(state), f64(action)], axis=-1)
    z = (mxq(xu, 1, "e4m3") @ mxq(f64(up_w1), 1, "e4m3").T) + f64(up_b1)
    t = np.tanh(l2norm(z))
    return np.tanh((mxq(t, 1, "e4m3") @ mxq(f64(up_w2_self), 1, "e4m3").T) + f64(up_b2))

@@ -1,0 +1,237 @@
+from contextlib import ExitStack
+
+import concourse.mybir as mybir
+from concourse.masks import make_identity
+
+F32 = mybir.dt.float32
+BF16 = mybir.dt.bfloat16
+U32 = mybir.dt.uint32
+U8 = mybir.dt.uint8
+FP8X4 = mybir.dt.float8_e4m3fn_x4
+ALU = mybir.AluOpType
+ACT = mybir.ActivationFunctionType
+
+P = 128
+PACK = 4
+K_PASS = P * PACK
+BATCH = 1024
+STATE = 896
+FEAT = 1024
+HID = 1024
+PASSES = FEAT // K_PASS
+N_TILE = 512
+HALVES = HID // N_TILE
+ROW_TILES = BATCH // P
+WORDS = FEAT // 2
+EPS = 1e-12
+W2_PER_STEP = 3
+T_STEP = 3
+OUT_STEP = 6
+
+FLOPS = 2 * BATCH * FEAT * HID + 2 * BATCH * HID * HID
+
+
+def w2_tiles_of_step(k):
+    return range(max(k - 1, 0) * W2_PER_STEP, min(k * W2_PER_STEP, ROW_TILES))
+
+
+def tile_modelgraphpolicy_pa_kernel(
+    tc, state, action, up_w1, up_b1, up_w2_self, up_b2, out
+):
+    nc = tc.nc
+    with ExitStack() as ctx:
+        ctx.enter_context(tc.manual_schedule())
+        keep = ctx.enter_context(tc.tile_pool(name="keep", bufs=1))
+        stage = ctx.enter_context(tc.tile_pool(name="stage", bufs=2))
+        flipped = ctx.enter_context(tc.psum_pool(name="flipped", bufs=4))
+        sums = ctx.enter_context(tc.psum_pool(name="sums", bufs=4))
+
+        ident = keep.tile([P, P], F32)
+        make_identity(nc, ident[:])
+        ones = keep.tile([P, P], BF16)
+        nc.gpsimd.memset(ones[:], 1.0)
+        neg_half = keep.tile([P, 1], F32)
+        nc.gpsimd.memset(neg_half[:], -0.5)
+        bias_rows = keep.tile([P, 2 * HID], BF16)
+        nc.vector.memset(bias_rows[:], 0.0)
+
+        nc.scalar.dma_start(
+            out=bias_rows[0:1, 0:HID], in_=up_b1.rearrange("(o h) -> o h", o=1)
+        )
+        nc.scalar.dma_start(
+            out=bias_rows[0:1, HID : 2 * HID], in_=up_b2.rearrange("(o h) -> o h", o=1)
+        )
+        warm = keep.tile([P, 1], F32)
+        nc.scalar.activation(out=warm[:], in_=neg_half[:], func=ACT.Tanh)
+
+        x_raw = keep.tile([P, ROW_TILES * FEAT], BF16)
+        w1_raw = keep.tile([P, ROW_TILES * FEAT], BF16)
+        w2_raw = keep.tile([P, ROW_TILES * FEAT], BF16)
+
+        def load_xu(i):
+            rows = slice(i * P, (i + 1) * P)
+            nc.sync.dma_start(out=x_raw[:, i * FEAT : i * FEAT + STATE], in_=state[rows, :])
+            nc.sync.dma_start(out=x_raw[:, i * FEAT + STATE : (i + 1) * FEAT], in_=action[rows, :])
+
+        def load_weight(raw, weight, j):
+            nc.sync.dma_start(
+                out=raw[:, j * FEAT : (j + 1) * FEAT], in_=weight[j * P : (j + 1) * P, :]
+            )
+
+        load_xu(0)
+        for j in range(ROW_TILES):
+            load_weight(w1_raw, up_w1, j)
+        for i in range(1, ROW_TILES):
+            load_xu(i)
+            for j in w2_tiles_of_step(i):
+                load_weight(w2_raw, up_w2_self, j)
+
+        x_codes = keep.tile([P, PASSES, BATCH], U32, align_bytes=64)
+        x_scales = keep.tile([P, PASSES, BATCH], U8, align_bytes=64)
+        w1_codes = keep.tile([P, PASSES, HID], U32, align_bytes=64)
+        w1_scales = keep.tile([P, PASSES, HID], U8, align_bytes=64)
+        w2_codes = keep.tile([P, PASSES, HID], U32, align_bytes=64)
+        w2_scales = keep.tile([P, PASSES, HID], U8, align_bytes=64)
+        t_codes = keep.tile([P, PASSES, BATCH], U32, align_bytes=64)
+        t_scales = keep.tile([P, PASSES, BATCH], U8, align_bytes=64)
+
+        def flip(raw, i):
+            words = raw[:].bitcast(F32)
+            bank = flipped.tile([P, PACK, P], F32, tag="bank")
+            for s in range(PACK):
+                first = i * WORDS + s * P
+                nc.tensor.transpose(
+                    out=bank[:, s, :], in_=words[:, first : first + P], identity=ident[:]
+                )
+            return bank
+
+        def regroup(copy, bank):
+            grouped = stage.tile([P, PASSES * K_PASS], BF16, align_bytes=64, tag="grouped", bufs=4)
+            copy(
+                out=grouped[:].bitcast(F32).rearrange("p (g r u) -> p g r u", g=PASSES, u=2),
+                in_=bank[:].rearrange("p (g u) r -> p g r u", g=PASSES),
+            )
+            return grouped
+
+        def quantise(grouped, codes, scales, tile_index):
+            cols = slice(tile_index * P, (tile_index + 1) * P)
+            for g in range(PASSES):
+                nc.vector.quantize_mx(
+                    out=codes[:, g, cols].bitcast(FP8X4),
+                    scales=scales[:, g, cols],
+                    in_=grouped[:, g * K_PASS : (g + 1) * K_PASS],
+                )
+
+        def mx_product(a_codes, a_scales, tile_index, w_codes, w_scales, half):
+            acc = sums.tile([P, N_TILE], F32, tag="acc")
+            rows = slice(tile_index * P, (tile_index + 1) * P)
+            cols = slice(half * N_TILE, (half + 1) * N_TILE)
+            for g in range(PASSES):
+                nc.tensor.matmul_mx(
+                    out=acc[:],
+                    lhsT=a_codes[:, g, rows].bitcast(FP8X4),
+                    lhsT_scale=a_scales[:, g, rows],
+                    rhs=w_codes[:, g, cols].bitcast(FP8X4),
+                    rhs_scale=w_scales[:, g, cols],
+                    start=(g == 0),
+                    stop=(g == PASSES - 1),
+                )
+            return acc
+
+        def prepare_w1(j):
+            grouped = regroup(nc.scalar.copy, flip(w1_raw, j))
+            quantise(grouped, w1_codes, w1_scales, j)
+
+        x_grouped = regroup(nc.vector.tensor_copy, flip(x_raw, 0))
+        quantise(x_grouped, x_codes, x_scales, 0)
+        for j in range(ROW_TILES // 2):
+            prepare_w1(j)
+        bias_all = keep.tile([P, 2 * HID], F32)
+        for c in range(2 * HALVES):
+            cols = slice(c * N_TILE, (c + 1) * N_TILE)
+            spread = sums.tile([P, N_TILE], F32, tag="acc")
+            nc.tensor.matmul(
+                out=spread[:], lhsT=ones[:], rhs=bias_rows[:, cols], start=True, stop=True
+            )
+            nc.vector.tensor_copy(out=bias_all[:, cols], in_=spread[:])
+        b1_all = bias_all[:, 0:HID]
+        b2_all = bias_all[:, HID : 2 * HID]
+        for j in range(ROW_TILES // 2, ROW_TILES):
+            prepare_w1(j)
+
+        sum_sq = keep.tile([P, ROW_TILES], F32)
+        floored = keep.tile([P, ROW_TILES], F32)
+        inv_norm = keep.tile([P, ROW_TILES], F32)
+        z_tiles = {}
+        t_tiles = {}
+
+        def live(i):
+            return 0 <= i < ROW_TILES
+
+        for k in range(1, ROW_TILES + OUT_STEP):
+            if live(k):
+                x_bank = flip(x_raw, k)
+            if live(k - T_STEP):
+                t_bank = flip(t_tiles[k - T_STEP], 0)
+            if live(k - 2):
+                t = stage.tile([P, HID], BF16, tag="t", bufs=3)
+                t_tiles[k - 2] = t
+                nc.scalar.activation(
+                    out=t[:],
+                    in_=z_tiles[k - 2][:],
+                    func=ACT.Tanh,
+                    scale=inv_norm[:, k - 2 : k - 1],
+                )
+            if live(k):
+                x_grouped = regroup(nc.vector.tensor_copy, x_bank)
+            if live(k - T_STEP):
+                t_copy = nc.scalar.copy if (k - T_STEP) % 2 == 0 else nc.vector.tensor_copy
+                t_grouped = regroup(t_copy, t_bank)
+
+            if live(k - 1):
+                z = stage.tile([P, HID], F32, tag="z", bufs=3)
+                z_tiles[k - 1] = z
+                for half in range(HALVES):
+                    cols = slice(half * N_TILE, (half + 1) * N_TILE)
+                    acc = mx_product(x_codes, x_scales, k - 1, w1_codes, w1_scales, half)
+                    nc.vector.tensor_tensor(
+                        out=z[:, cols], in0=acc[:], in1=b1_all[:, cols], op=ALU.add
+                    )
+                squares = stage.tile([P, HID], BF16, tag="squares")
+                nc.scalar.activation(
+                    out=squares[:], in_=z[:], func=ACT.Square, accum_out=sum_sq[:, k - 1 : k]
+                )
+                nc.gpsimd.tensor_scalar(
+                    out=floored[:, k - 1 : k],
+                    in0=sum_sq[:, k - 1 : k],
+                    scalar1=EPS * EPS,
+                    scalar2=None,
+                    op0=ALU.max,
+                )
+                nc.gpsimd.tensor_tensor(
+                    out=inv_norm[:, k - 1 : k],
+                    in0=floored[:, k - 1 : k],
+                    in1=neg_half[:],
+                    op=ALU.pow,
+                )
+            if live(k):
+                quantise(x_grouped, x_codes, x_scales, k)
+
+            if live(k - OUT_STEP):
+                i = k - OUT_STEP
+                for half in range(HALVES):
+                    cols = slice(half * N_TILE, (half + 1) * N_TILE)
+                    acc = mx_product(t_codes, t_scales, i, w2_codes, w2_scales, half)
+                    result = stage.tile([P, N_TILE], F32, tag="result", bufs=6)
+                    nc.vector.tensor_tensor(
+                        out=result[:], in0=acc[:], in1=b2_all[:, cols], op=ALU.add
+                    )
+                    nc.scalar.activation(out=result[:], in_=result[:], func=ACT.Tanh)
+                    nc.sync.dma_start(out=out[i * P : (i + 1) * P, cols], in_=result[:])
+            if live(k - T_STEP):
+                quantise(t_grouped, t_codes, t_scales, k - T_STEP)
+
+            w2_banks = [flip(w2_raw, j) for j in w2_tiles_of_step(k)]
+            w2_grouped = [regroup(nc.scalar.copy, bank) for bank in w2_banks]
+            for j, grouped in zip(w2_tiles_of_step(k), w2_grouped):
+                quantise(grouped, w2_codes, w2_scales, j)

@@ -24,15 +24,9 @@ HALVES = HID // N_TILE
 ROW_TILES = BATCH // P
 WORDS = FEAT // 2
 EPS = 1e-12
-W2_PER_STEP = 3
-T_STEP = 3
-OUT_STEP = 6
+OUT_LAG = 3
 
 FLOPS = 2 * BATCH * FEAT * HID + 2 * BATCH * HID * HID
-
-
-def w2_tiles_of_step(k):
-    return range(max(k - 1, 0) * W2_PER_STEP, min(k * W2_PER_STEP, ROW_TILES))
 
 
 def tile_modelgraphpolicy_pa_kernel(
@@ -81,10 +75,11 @@ def tile_modelgraphpolicy_pa_kernel(
         load_xu(0)
         for j in range(ROW_TILES):
             load_weight(w1_raw, up_w1, j)
-        for i in range(1, ROW_TILES):
-            load_xu(i)
-            for j in w2_tiles_of_step(i):
-                load_weight(w2_raw, up_w2_self, j)
+        load_xu(1)
+        for i in range(ROW_TILES):
+            load_weight(w2_raw, up_w2_self, i)
+            if i + 2 < ROW_TILES:
+                load_xu(i + 2)
 
         x_codes = keep.tile([P, PASSES, BATCH], U32, align_bytes=64)
         x_scales = keep.tile([P, PASSES, BATCH], U8, align_bytes=64)
@@ -158,80 +153,71 @@ def tile_modelgraphpolicy_pa_kernel(
         b2_all = bias_all[:, HID : 2 * HID]
         for j in range(ROW_TILES // 2, ROW_TILES):
             prepare_w1(j)
+        x_grouped = regroup(nc.vector.tensor_copy, flip(x_raw, 1))
 
+        z_all = keep.tile([P, ROW_TILES, HID], F32)
         sum_sq = keep.tile([P, ROW_TILES], F32)
         floored = keep.tile([P, ROW_TILES], F32)
         inv_norm = keep.tile([P, ROW_TILES], F32)
-        z_tiles = {}
+
+        def norm(i):
+            squares = stage.tile([P, HID], BF16, tag="squares")
+            nc.scalar.activation(
+                out=squares[:], in_=z_all[:, i, :], func=ACT.Square, accum_out=sum_sq[:, i : i + 1]
+            )
+            nc.gpsimd.tensor_scalar(
+                out=floored[:, i : i + 1],
+                in0=sum_sq[:, i : i + 1],
+                scalar1=EPS * EPS,
+                scalar2=None,
+                op0=ALU.max,
+            )
+            nc.gpsimd.tensor_tensor(
+                out=inv_norm[:, i : i + 1], in0=floored[:, i : i + 1], in1=neg_half[:], op=ALU.pow
+            )
+
+        for i in range(ROW_TILES):
+            if i + 1 < ROW_TILES:
+                quantise(x_grouped, x_codes, x_scales, i + 1)
+            for half in range(HALVES):
+                cols = slice(half * N_TILE, (half + 1) * N_TILE)
+                acc = mx_product(x_codes, x_scales, i, w1_codes, w1_scales, half)
+                nc.vector.tensor_tensor(
+                    out=z_all[:, i, cols], in0=acc[:], in1=b1_all[:, cols], op=ALU.add
+                )
+            w2_grouped = regroup(nc.scalar.copy, flip(w2_raw, i))
+            if i + 2 < ROW_TILES:
+                x_copy = nc.scalar.copy if i % 2 == 0 else nc.vector.tensor_copy
+                x_grouped = regroup(x_copy, flip(x_raw, i + 2))
+            if i > 0:
+                norm(i - 1)
+            quantise(w2_grouped, w2_codes, w2_scales, i)
+        norm(ROW_TILES - 1)
+
         t_tiles = {}
 
         def live(i):
             return 0 <= i < ROW_TILES
 
-        for k in range(1, ROW_TILES + OUT_STEP):
-            if live(k):
-                x_bank = flip(x_raw, k)
-            if live(k - T_STEP):
-                t_bank = flip(t_tiles[k - T_STEP], 0)
-            if live(k - 2):
+        for i in range(ROW_TILES + OUT_LAG):
+            if live(i):
                 t = stage.tile([P, HID], BF16, tag="t", bufs=3)
-                t_tiles[k - 2] = t
+                t_tiles[i] = t
                 nc.scalar.activation(
-                    out=t[:],
-                    in_=z_tiles[k - 2][:],
-                    func=ACT.Tanh,
-                    scale=inv_norm[:, k - 2 : k - 1],
+                    out=t[:], in_=z_all[:, i, :], func=ACT.Tanh, scale=inv_norm[:, i : i + 1]
                 )
-            if live(k):
-                x_grouped = regroup(nc.vector.tensor_copy, x_bank)
-            if live(k - T_STEP):
-                t_copy = nc.scalar.copy if (k - T_STEP) % 2 == 0 else nc.vector.tensor_copy
-                t_grouped = regroup(t_copy, t_bank)
-
-            if live(k - 1):
-                z = stage.tile([P, HID], F32, tag="z", bufs=3)
-                z_tiles[k - 1] = z
+            if live(i - 1):
+                t_grouped = regroup(nc.vector.tensor_copy, flip(t_tiles[i - 1], 0))
+            if live(i - OUT_LAG):
+                rows = slice((i - OUT_LAG) * P, (i - OUT_LAG + 1) * P)
                 for half in range(HALVES):
                     cols = slice(half * N_TILE, (half + 1) * N_TILE)
-                    acc = mx_product(x_codes, x_scales, k - 1, w1_codes, w1_scales, half)
-                    nc.vector.tensor_tensor(
-                        out=z[:, cols], in0=acc[:], in1=b1_all[:, cols], op=ALU.add
-                    )
-                squares = stage.tile([P, HID], BF16, tag="squares")
-                nc.scalar.activation(
-                    out=squares[:], in_=z[:], func=ACT.Square, accum_out=sum_sq[:, k - 1 : k]
-                )
-                nc.gpsimd.tensor_scalar(
-                    out=floored[:, k - 1 : k],
-                    in0=sum_sq[:, k - 1 : k],
-                    scalar1=EPS * EPS,
-                    scalar2=None,
-                    op0=ALU.max,
-                )
-                nc.gpsimd.tensor_tensor(
-                    out=inv_norm[:, k - 1 : k],
-                    in0=floored[:, k - 1 : k],
-                    in1=neg_half[:],
-                    op=ALU.pow,
-                )
-            if live(k):
-                quantise(x_grouped, x_codes, x_scales, k)
-
-            if live(k - OUT_STEP):
-                i = k - OUT_STEP
-                for half in range(HALVES):
-                    cols = slice(half * N_TILE, (half + 1) * N_TILE)
-                    acc = mx_product(t_codes, t_scales, i, w2_codes, w2_scales, half)
+                    acc = mx_product(t_codes, t_scales, i - OUT_LAG, w2_codes, w2_scales, half)
                     result = stage.tile([P, N_TILE], F32, tag="result", bufs=6)
                     nc.vector.tensor_tensor(
                         out=result[:], in0=acc[:], in1=b2_all[:, cols], op=ALU.add
                     )
                     nc.scalar.activation(out=result[:], in_=result[:], func=ACT.Tanh)
-                    nc.sync.dma_start(out=out[i * P : (i + 1) * P, cols], in_=result[:])
-            if live(k - T_STEP):
-                quantise(t_grouped, t_codes, t_scales, k - T_STEP)
-
-            w2_banks = [flip(w2_raw, j) for j in w2_tiles_of_step(k)]
-            w2_grouped = [regroup(nc.scalar.copy, bank) for bank in w2_banks]
-            for j, grouped in zip(w2_tiles_of_step(k), w2_grouped):
-                quantise(grouped, w2_codes, w2_scales, j)
+                    nc.sync.dma_start(out=out[rows, cols], in_=result[:])
+            if live(i - 1):
+                quantise(t_grouped, t_codes, t_scales, i - 1)

@@ -34,7 +34,6 @@ def tile_modelgraphpolicy_pa_kernel(
 ):
     nc = tc.nc
     with ExitStack() as ctx:
-        ctx.enter_context(tc.manual_schedule())
         keep = ctx.enter_context(tc.tile_pool(name="keep", bufs=1))
         stage = ctx.enter_context(tc.tile_pool(name="stage", bufs=2))
         flipped = ctx.enter_context(tc.psum_pool(name="flipped", bufs=4))

@@ -136,23 +136,24 @@ def tile_modelgraphpolicy_pa_kernel(
             grouped = regroup(nc.scalar.copy, flip(w1_raw, j))
             quantise(grouped, w1_codes, w1_scales, j)
 
-        x_grouped = regroup(nc.vector.tensor_copy, flip(x_raw, 0))
-        quantise(x_grouped, x_codes, x_scales, 0)
-        for j in range(ROW_TILES // 2):
-            prepare_w1(j)
-        bias_all = keep.tile([P, 2 * HID], F32)
-        for c in range(2 * HALVES):
-            cols = slice(c * N_TILE, (c + 1) * N_TILE)
-            spread = sums.tile([P, N_TILE], F32, tag="acc")
-            nc.tensor.matmul(
-                out=spread[:], lhsT=ones[:], rhs=bias_rows[:, cols], start=True, stop=True
-            )
-            nc.vector.tensor_copy(out=bias_all[:, cols], in_=spread[:])
-        b1_all = bias_all[:, 0:HID]
-        b2_all = bias_all[:, HID : 2 * HID]
-        for j in range(ROW_TILES // 2, ROW_TILES):
-            prepare_w1(j)
-        x_grouped = regroup(nc.vector.tensor_copy, flip(x_raw, 1))
+        with tc.manual_schedule():
+            x_grouped = regroup(nc.vector.tensor_copy, flip(x_raw, 0))
+            quantise(x_grouped, x_codes, x_scales, 0)
+            for j in range(ROW_TILES // 2):
+                prepare_w1(j)
+            bias_all = keep.tile([P, 2 * HID], F32)
+            for c in range(2 * HALVES):
+                cols = slice(c * N_TILE, (c + 1) * N_TILE)
+                spread = sums.tile([P, N_TILE], F32, tag="acc")
+                nc.tensor.matmul(
+                    out=spread[:], lhsT=ones[:], rhs=bias_rows[:, cols], start=True, stop=True
+                )
+                nc.vector.tensor_copy(out=bias_all[:, cols], in_=spread[:])
+            b1_all = bias_all[:, 0:HID]
+            b2_all = bias_all[:, HID : 2 * HID]
+            for j in range(ROW_TILES // 2, ROW_TILES):
+                prepare_w1(j)
+            x_grouped = regroup(nc.vector.tensor_copy, flip(x_raw, 1))
 
         z_all = keep.tile([P, ROW_TILES, HID], F32)
         sum_sq = keep.tile([P, ROW_TILES], F32)

@@ -24,7 +24,6 @@ HALVES = HID // N_TILE
 ROW_TILES = BATCH // P
 WORDS = FEAT // 2
 EPS = 1e-12
-OUT_LAG = 3
 
 FLOPS = 2 * BATCH * FEAT * HID + 2 * BATCH * HID * HID
 
@@ -38,6 +37,7 @@ def tile_modelgraphpolicy_pa_kernel(
         stage = ctx.enter_context(tc.tile_pool(name="stage", bufs=2))
         flipped = ctx.enter_context(tc.psum_pool(name="flipped", bufs=4))
         sums = ctx.enter_context(tc.psum_pool(name="sums", bufs=4))
+        ctx.enter_context(tc.manual_schedule())
 
         ident = keep.tile([P, P], F32)
         make_identity(nc, ident[:])
@@ -45,17 +45,17 @@ def tile_modelgraphpolicy_pa_kernel(
         nc.gpsimd.memset(ones[:], 1.0)
         neg_half = keep.tile([P, 1], F32)
         nc.gpsimd.memset(neg_half[:], -0.5)
-        bias_rows = keep.tile([P, 2 * HID], BF16)
-        nc.vector.memset(bias_rows[:], 0.0)
+        b1_rows = keep.tile([P, HID], BF16)
+        nc.vector.memset(b1_rows[:], 0.0)
+        b2_rows = keep.tile([P, HID], BF16)
+        nc.vector.memset(b2_rows[:], 0.0)
 
         nc.scalar.dma_start(
-            out=bias_rows[0:1, 0:HID], in_=up_b1.rearrange("(o h) -> o h", o=1)
-        )
-        nc.scalar.dma_start(
-            out=bias_rows[0:1, HID : 2 * HID], in_=up_b2.rearrange("(o h) -> o h", o=1)
+            out=b1_rows[0:1, :], in_=up_b1.rearrange("(o h) -> o h", o=1)
         )
         warm = keep.tile([P, 1], F32)
         nc.scalar.activation(out=warm[:], in_=neg_half[:], func=ACT.Tanh)
+        nc.scalar.dma_start(out=b2_rows[0:1, :], in_=up_b2.rearrange("(o h) -> o h", o=1))
 
         x_raw = keep.tile([P, ROW_TILES * FEAT], BF16)
         w1_raw = keep.tile([P, ROW_TILES * FEAT], BF16)
@@ -72,13 +72,15 @@ def tile_modelgraphpolicy_pa_kernel(
             )
 
         load_xu(0)
-        for j in range(ROW_TILES):
+        for j in range(ROW_TILES // 2):
             load_weight(w1_raw, up_w1, j)
         load_xu(1)
+        for j in range(ROW_TILES // 2, ROW_TILES):
+            load_weight(w1_raw, up_w1, j)
         for i in range(ROW_TILES):
-            load_weight(w2_raw, up_w2_self, i)
             if i + 2 < ROW_TILES:
                 load_xu(i + 2)
+            load_weight(w2_raw, up_w2_self, i)
 
         x_codes = keep.tile([P, PASSES, BATCH], U32, align_bytes=64)
         x_scales = keep.tile([P, PASSES, BATCH], U8, align_bytes=64)
@@ -100,7 +102,7 @@ def tile_modelgraphpolicy_pa_kernel(
             return bank
 
         def regroup(copy, bank):
-            grouped = stage.tile([P, PASSES * K_PASS], BF16, align_bytes=64, tag="grouped", bufs=4)
+            grouped = stage.tile([P, PASSES * K_PASS], BF16, align_bytes=64, tag="grouped", bufs=6)
             copy(
                 out=grouped[:].bitcast(F32).rearrange("p (g r u) -> p g r u", g=PASSES, u=2),
                 in_=bank[:].rearrange("p (g u) r -> p g r u", g=PASSES),
@@ -132,33 +134,46 @@ def tile_modelgraphpolicy_pa_kernel(
                 )
             return acc
 
-        def prepare_w1(j):
-            grouped = regroup(nc.scalar.copy, flip(w1_raw, j))
-            quantise(grouped, w1_codes, w1_scales, j)
-
-        with tc.manual_schedule():
-            x_grouped = regroup(nc.vector.tensor_copy, flip(x_raw, 0))
-            quantise(x_grouped, x_codes, x_scales, 0)
-            for j in range(ROW_TILES // 2):
-                prepare_w1(j)
-            bias_all = keep.tile([P, 2 * HID], F32)
-            for c in range(2 * HALVES):
+        def spread_bias(rows):
+            everywhere = keep.tile([P, HID], BF16, tag="everywhere", bufs=2)
+            for c in range(HALVES):
                 cols = slice(c * N_TILE, (c + 1) * N_TILE)
-                spread = sums.tile([P, N_TILE], F32, tag="acc")
+                spread = sums.tile([P, N_TILE], BF16, tag="acc")
                 nc.tensor.matmul(
-                    out=spread[:], lhsT=ones[:], rhs=bias_rows[:, cols], start=True, stop=True
+                    out=spread[:], lhsT=ones[:], rhs=rows[:, cols], start=True, stop=True
                 )
-                nc.vector.tensor_copy(out=bias_all[:, cols], in_=spread[:])
-            b1_all = bias_all[:, 0:HID]
-            b2_all = bias_all[:, HID : 2 * HID]
-            for j in range(ROW_TILES // 2, ROW_TILES):
-                prepare_w1(j)
-            x_grouped = regroup(nc.vector.tensor_copy, flip(x_raw, 1))
+                nc.vector.tensor_copy(out=everywhere[:, cols], in_=spread[:])
+            return everywhere
 
         z_all = keep.tile([P, ROW_TILES, HID], F32)
+        t_all = keep.tile([P, ROW_TILES * HID], BF16)
         sum_sq = keep.tile([P, ROW_TILES], F32)
         floored = keep.tile([P, ROW_TILES], F32)
         inv_norm = keep.tile([P, ROW_TILES], F32)
+        raws = {"x": x_raw, "w1": w1_raw, "w2": w2_raw, "t": t_all}
+        codes = {"x": x_codes, "w1": w1_codes, "w2": w2_codes, "t": t_codes}
+        scales = {"x": x_scales, "w1": w1_scales, "w2": w2_scales, "t": t_scales}
+        grouped = {}
+
+        def turn(operand, i, copy):
+            grouped[operand, i] = regroup(copy, flip(raws[operand], i))
+
+        def pack(operand, i):
+            quantise(grouped[operand, i], codes[operand], scales[operand], i)
+
+        on_scalar = nc.scalar.copy
+        on_vector = nc.vector.tensor_copy
+        first = {}
+        second = {}
+
+        def first_layer(i, half):
+            first[i, half] = mx_product(x_codes, x_scales, i, w1_codes, w1_scales, half)
+
+        def add_b1(i, half):
+            cols = slice(half * N_TILE, (half + 1) * N_TILE)
+            nc.vector.tensor_tensor(
+                out=z_all[:, i, cols], in0=first[i, half][:], in1=b1_all[:, cols], op=ALU.add
+            )
 
         def norm(i):
             squares = stage.tile([P, HID], BF16, tag="squares")
@@ -176,48 +191,95 @@ def tile_modelgraphpolicy_pa_kernel(
                 out=inv_norm[:, i : i + 1], in0=floored[:, i : i + 1], in1=neg_half[:], op=ALU.pow
             )
 
+        def hidden(i):
+            nc.scalar.activation(
+                out=t_all[:, i * HID : (i + 1) * HID],
+                in_=z_all[:, i, :],
+                func=ACT.Tanh,
+                scale=inv_norm[:, i : i + 1],
+            )
+
+        def second_layer(i, half):
+            second[i, half] = mx_product(t_codes, t_scales, i, w2_codes, w2_scales, half)
+
+        results = {}
+
+        def add_b2(i, half):
+            cols = slice(half * N_TILE, (half + 1) * N_TILE)
+            result = stage.tile([P, N_TILE], F32, tag="result", bufs=6)
+            results[i, half] = result
+            nc.vector.tensor_tensor(
+                out=result[:], in0=second[i, half][:], in1=b2_all[:, cols], op=ALU.add
+            )
+
+        def finish(i, half):
+            rows = slice(i * P, (i + 1) * P)
+            cols = slice(half * N_TILE, (half + 1) * N_TILE)
+            result = results[i, half]
+            nc.scalar.activation(out=result[:], in_=result[:], func=ACT.Tanh)
+            nc.sync.dma_start(out=out[rows, cols], in_=result[:])
+
+        b1_all = spread_bias(b1_rows)
+        turn("x", 0, on_vector)
+        turn("w1", 0, on_scalar)
+        pack("x", 0)
+        for j in range(1, ROW_TILES // 2):
+            turn("w1", j, on_scalar)
+            pack("w1", j - 1)
+        turn("x", 1, on_scalar)
+        pack("w1", 3)
+        turn("w1", 4, on_scalar)
+        pack("x", 1)
+        turn("w1", 5, on_scalar)
+        pack("w1", 4)
+        first_layer(0, 0)
+        add_b1(0, 0)
+        turn("w1", 6, on_scalar)
+        pack("w1", 5)
+        turn("w1", 7, on_scalar)
+        pack("w1", 6)
+        first_layer(1, 0)
+        add_b1(1, 0)
+        turn("x", 2, on_scalar)
+        pack("w1", 7)
+        turn("w2", 0, on_scalar)
+
         for i in range(ROW_TILES):
-            if i + 1 < ROW_TILES:
-                quantise(x_grouped, x_codes, x_scales, i + 1)
-            for half in range(HALVES):
-                cols = slice(half * N_TILE, (half + 1) * N_TILE)
-                acc = mx_product(x_codes, x_scales, i, w1_codes, w1_scales, half)
-                nc.vector.tensor_tensor(
-                    out=z_all[:, i, cols], in0=acc[:], in1=b1_all[:, cols], op=ALU.add
-                )
-            w2_grouped = regroup(nc.scalar.copy, flip(w2_raw, i))
-            if i + 2 < ROW_TILES:
-                x_copy = nc.scalar.copy if i % 2 == 0 else nc.vector.tensor_copy
-                x_grouped = regroup(x_copy, flip(x_raw, i + 2))
+            halves = range(HALVES) if i > 1 else range(1, HALVES)
+            for half in halves:
+                first_layer(i, half)
             if i > 0:
                 norm(i - 1)
-            quantise(w2_grouped, w2_codes, w2_scales, i)
+            if i + 1 < ROW_TILES:
+                turn("w2", i + 1, on_scalar)
+            if i + 2 < ROW_TILES:
+                pack("x", i + 2)
+            for half in halves:
+                add_b1(i, half)
+            pack("w2", i)
+            if i + 3 < ROW_TILES:
+                turn("x", i + 3, on_vector if (i + 3) % 2 == 1 else on_scalar)
+            if i == 5:
+                b2_all = spread_bias(b2_rows)
+            if i >= 4:
+                hidden(i - 4)
+            if i == 6:
+                turn("t", 0, on_vector)
+            if i == 7:
+                pack("t", 0)
+                turn("t", 1, on_vector)
         norm(ROW_TILES - 1)
 
-        t_tiles = {}
-
-        def live(i):
-            return 0 <= i < ROW_TILES
-
-        for i in range(ROW_TILES + OUT_LAG):
-            if live(i):
-                t = stage.tile([P, HID], BF16, tag="t", bufs=3)
-                t_tiles[i] = t
-                nc.scalar.activation(
-                    out=t[:], in_=z_all[:, i, :], func=ACT.Tanh, scale=inv_norm[:, i : i + 1]
-                )
-            if live(i - 1):
-                t_grouped = regroup(nc.vector.tensor_copy, flip(t_tiles[i - 1], 0))
-            if live(i - OUT_LAG):
-                rows = slice((i - OUT_LAG) * P, (i - OUT_LAG + 1) * P)
-                for half in range(HALVES):
-                    cols = slice(half * N_TILE, (half + 1) * N_TILE)
-                    acc = mx_product(t_codes, t_scales, i - OUT_LAG, w2_codes, w2_scales, half)
-                    result = stage.tile([P, N_TILE], F32, tag="result", bufs=6)
-                    nc.vector.tensor_tensor(
-                        out=result[:], in0=acc[:], in1=b2_all[:, cols], op=ALU.add
-                    )
-                    nc.scalar.activation(out=result[:], in_=result[:], func=ACT.Tanh)
-                    nc.sync.dma_start(out=out[rows, cols], in_=result[:])
-            if live(i - 1):
-                quantise(t_grouped, t_codes, t_scales, i - 1)
+        for i in range(ROW_TILES):
+            for half in range(HALVES):
+                second_layer(i, half)
+            add_b2(i, 0)
+            if i + 1 < ROW_TILES:
+                pack("t", i + 1)
+            add_b2(i, 1)
+            if i + 2 < ROW_TILES:
+                turn("t", i + 2, on_vector)
+            if i + 4 < ROW_TILES:
+                hidden(i + 4)
+            for half in range(HALVES):
+                finish(i, half)

@@ -55,7 +55,6 @@ def tile_modelgraphpolicy_pa_kernel(
         )
         warm = keep.tile([P, 1], F32)
         nc.scalar.activation(out=warm[:], in_=neg_half[:], func=ACT.Tanh)
-        nc.scalar.dma_start(out=b2_rows[0:1, :], in_=up_b2.rearrange("(o h) -> o h", o=1))
 
         x_raw = keep.tile([P, ROW_TILES * FEAT], BF16)
         w1_raw = keep.tile([P, ROW_TILES * FEAT], BF16)
@@ -81,6 +80,7 @@ def tile_modelgraphpolicy_pa_kernel(
             if i + 2 < ROW_TILES:
                 load_xu(i + 2)
             load_weight(w2_raw, up_w2_self, i)
+        nc.sync.dma_start(out=b2_rows[0:1, :], in_=up_b2.rearrange("(o h) -> o h", o=1))
 
         x_codes = keep.tile([P, PASSES, BATCH], U32, align_bytes=64)
         x_scales = keep.tile([P, PASSES, BATCH], U8, align_bytes=64)
@@ -219,7 +219,6 @@ def tile_modelgraphpolicy_pa_kernel(
             nc.scalar.activation(out=result[:], in_=result[:], func=ACT.Tanh)
             nc.sync.dma_start(out=out[rows, cols], in_=result[:])
 
-        b1_all = spread_bias(b1_rows)
         turn("x", 0, on_vector)
         turn("w1", 0, on_scalar)
         pack("x", 0)
@@ -232,6 +231,7 @@ def tile_modelgraphpolicy_pa_kernel(
         pack("x", 1)
         turn("w1", 5, on_scalar)
         pack("w1", 4)
+        b1_all = spread_bias(b1_rows)
         first_layer(0, 0)
         add_b1(0, 0)
         turn("w1", 6, on_scalar)

@@ -71,11 +71,9 @@ def tile_modelgraphpolicy_pa_kernel(
             )
 
         load_xu(0)
-        for j in range(ROW_TILES // 2):
+        for j in range(ROW_TILES):
             load_weight(w1_raw, up_w1, j)
         load_xu(1)
-        for j in range(ROW_TILES // 2, ROW_TILES):
-            load_weight(w1_raw, up_w1, j)
         for i in range(ROW_TILES):
             if i + 2 < ROW_TILES:
                 load_xu(i + 2)
@@ -102,7 +100,7 @@ def tile_modelgraphpolicy_pa_kernel(
             return bank
 
         def regroup(copy, bank):
-            grouped = stage.tile([P, PASSES * K_PASS], BF16, align_bytes=64, tag="grouped", bufs=6)
+            grouped = stage.tile([P, PASSES * K_PASS], BF16, align_bytes=64, tag="grouped", bufs=8)
             copy(
                 out=grouped[:].bitcast(F32).rearrange("p (g r u) -> p g r u", g=PASSES, u=2),
                 in_=bank[:].rearrange("p (g u) r -> p g r u", g=PASSES),
@@ -155,8 +153,17 @@ def tile_modelgraphpolicy_pa_kernel(
         scales = {"x": x_scales, "w1": w1_scales, "w2": w2_scales, "t": t_scales}
         grouped = {}
 
+        banks = {}
+
+        def lift(operand, i):
+            banks[operand, i] = flip(raws[operand], i)
+
+        def settle(operand, i, copy):
+            grouped[operand, i] = regroup(copy, banks[operand, i])
+
         def turn(operand, i, copy):
-            grouped[operand, i] = regroup(copy, flip(raws[operand], i))
+            lift(operand, i)
+            settle(operand, i, copy)
 
         def pack(operand, i):
             quantise(grouped[operand, i], codes[operand], scales[operand], i)
@@ -206,7 +213,7 @@ def tile_modelgraphpolicy_pa_kernel(
 
         def add_b2(i, half):
             cols = slice(half * N_TILE, (half + 1) * N_TILE)
-            result = stage.tile([P, N_TILE], F32, tag="result", bufs=6)
+            result = stage.tile([P, N_TILE], F32, tag="result", bufs=8)
             results[i, half] = result
             nc.vector.tensor_tensor(
                 out=result[:], in0=second[i, half][:], in1=b2_all[:, cols], op=ALU.add
@@ -219,67 +226,69 @@ def tile_modelgraphpolicy_pa_kernel(
             nc.scalar.activation(out=result[:], in_=result[:], func=ACT.Tanh)
             nc.sync.dma_start(out=out[rows, cols], in_=result[:])
 
-        turn("x", 0, on_vector)
-        turn("w1", 0, on_scalar)
-        pack("x", 0)
-        for j in range(1, ROW_TILES // 2):
+        def turn_x(i):
+            turn("x", i, on_vector if i % 3 == 0 else on_scalar)
+
+        turn_x(0)
+        for j in range(ROW_TILES):
             turn("w1", j, on_scalar)
-            pack("w1", j - 1)
-        turn("x", 1, on_scalar)
-        pack("w1", 3)
-        turn("w1", 4, on_scalar)
+            if j == 0:
+                pack("x", 0)
+            else:
+                pack("w1", j - 1)
+            if j == ROW_TILES // 2:
+                b1_all = spread_bias(b1_rows)
+        turn_x(1)
+        pack("w1", ROW_TILES - 1)
+        turn_x(2)
         pack("x", 1)
-        turn("w1", 5, on_scalar)
-        pack("w1", 4)
-        b1_all = spread_bias(b1_rows)
-        first_layer(0, 0)
-        add_b1(0, 0)
-        turn("w1", 6, on_scalar)
-        pack("w1", 5)
-        turn("w1", 7, on_scalar)
-        pack("w1", 6)
-        first_layer(1, 0)
-        add_b1(1, 0)
-        turn("x", 2, on_scalar)
-        pack("w1", 7)
         turn("w2", 0, on_scalar)
+        pack("x", 2)
+        turn_x(3)
+        pack("w2", 0)
 
         for i in range(ROW_TILES):
-            halves = range(HALVES) if i > 1 else range(1, HALVES)
-            for half in halves:
+            if i + 1 < ROW_TILES:
+                lift("w2", i + 1)
+            new_x = i + 3 if 0 < i and i + 3 < ROW_TILES else None
+            if new_x:
+                lift("x", new_x)
+            for half in range(HALVES):
                 first_layer(i, half)
+            if i >= 3:
+                hidden(i - 3)
+            if i + 1 < ROW_TILES:
+                settle("w2", i + 1, on_scalar)
+            if new_x and new_x % 3 != 0:
+                settle("x", new_x, on_scalar)
             if i > 0:
                 norm(i - 1)
-            if i + 1 < ROW_TILES:
-                turn("w2", i + 1, on_scalar)
-            if i + 2 < ROW_TILES:
+            if 0 < i and i + 2 < ROW_TILES:
                 pack("x", i + 2)
-            for half in halves:
+            if new_x and new_x % 3 == 0:
+                settle("x", new_x, on_vector)
+            if i > 0:
+                pack("w2", i)
+            for half in range(HALVES):
                 add_b1(i, half)
-            pack("w2", i)
-            if i + 3 < ROW_TILES:
-                turn("x", i + 3, on_vector if (i + 3) % 2 == 1 else on_scalar)
-            if i == 5:
+            if i == 3:
                 b2_all = spread_bias(b2_rows)
             if i >= 4:
-                hidden(i - 4)
-            if i == 6:
-                turn("t", 0, on_vector)
-            if i == 7:
-                pack("t", 0)
-                turn("t", 1, on_vector)
+                turn("t", i - 4, on_vector)
+            if i >= 5:
+                pack("t", i - 5)
         norm(ROW_TILES - 1)
 
         for i in range(ROW_TILES):
+            if i + 5 < ROW_TILES:
+                hidden(i + 5)
             for half in range(HALVES):
                 second_layer(i, half)
             add_b2(i, 0)
-            if i + 1 < ROW_TILES:
-                pack("t", i + 1)
+            if 0 < i and i + 3 < ROW_TILES:
+                turn("t", i + 3, on_vector)
+            if 0 < i and i + 2 < ROW_TILES:
+                pack("t", i + 2)
             add_b2(i, 1)
-            if i + 2 < ROW_TILES:
-                turn("t", i + 2, on_vector)
-            if i + 4 < ROW_TILES:
-                hidden(i + 4)
             for half in range(HALVES):
                 finish(i, half)

@@ -41,18 +41,19 @@ def tile_modelgraphpolicy_pa_kernel(
 
         ident = keep.tile([P, P], F32)
         make_identity(nc, ident[:])
-        ones = keep.tile([P, P], BF16)
+        ones = keep.tile([P, N_TILE], BF16)
         nc.gpsimd.memset(ones[:], 1.0)
         neg_half = keep.tile([P, 1], F32)
         nc.gpsimd.memset(neg_half[:], -0.5)
         b1_rows = keep.tile([P, HID], BF16)
-        nc.vector.memset(b1_rows[:], 0.0)
+        nc.vector.memset(b1_rows[:].bitcast(U32), 0)
         b2_rows = keep.tile([P, HID], BF16)
-        nc.vector.memset(b2_rows[:], 0.0)
+        nc.vector.memset(b2_rows[:].bitcast(U32), 0)
 
         nc.scalar.dma_start(
             out=b1_rows[0:1, :], in_=up_b1.rearrange("(o h) -> o h", o=1)
         )
+        nc.scalar.dma_start(out=b2_rows[0:1, :], in_=up_b2.rearrange("(o h) -> o h", o=1))
         warm = keep.tile([P, 1], F32)
         nc.scalar.activation(out=warm[:], in_=neg_half[:], func=ACT.Tanh)
 
@@ -78,7 +79,6 @@ def tile_modelgraphpolicy_pa_kernel(
             if i + 2 < ROW_TILES:
                 load_xu(i + 2)
             load_weight(w2_raw, up_w2_self, i)
-        nc.sync.dma_start(out=b2_rows[0:1, :], in_=up_b2.rearrange("(o h) -> o h", o=1))
 
         x_codes = keep.tile([P, PASSES, BATCH], U32, align_bytes=64)
         x_scales = keep.tile([P, PASSES, BATCH], U8, align_bytes=64)
@@ -132,16 +132,11 @@ def tile_modelgraphpolicy_pa_kernel(
                 )
             return acc
 
-        def spread_bias(rows):
-            everywhere = keep.tile([P, HID], BF16, tag="everywhere", bufs=2)
-            for c in range(HALVES):
-                cols = slice(c * N_TILE, (c + 1) * N_TILE)
-                spread = sums.tile([P, N_TILE], BF16, tag="acc")
-                nc.tensor.matmul(
-                    out=spread[:], lhsT=ones[:], rhs=rows[:, cols], start=True, stop=True
-                )
-                nc.vector.tensor_copy(out=everywhere[:, cols], in_=spread[:])
-            return everywhere
+        def spread_bias(everywhere, rows, half):
+            cols = slice(half * N_TILE, (half + 1) * N_TILE)
+            spread = sums.tile([P, N_TILE], BF16, tag="acc")
+            nc.tensor.matmul(out=spread[:], lhsT=ones[:, 0:P], rhs=rows[:, cols], start=True, stop=True)
+            nc.vector.tensor_copy(out=everywhere[:, cols], in_=spread[:])
 
         z_all = keep.tile([P, ROW_TILES, HID], F32)
         t_all = keep.tile([P, ROW_TILES * HID], BF16)
@@ -167,6 +162,9 @@ def tile_modelgraphpolicy_pa_kernel(
 
         def pack(operand, i):
             quantise(grouped[operand, i], codes[operand], scales[operand], i)
+
+        b1_all = keep.tile([P, HID], BF16)
+        b2_all = keep.tile([P, HID], BF16)
 
         on_scalar = nc.scalar.copy
         on_vector = nc.vector.tensor_copy
@@ -226,69 +224,88 @@ def tile_modelgraphpolicy_pa_kernel(
             nc.scalar.activation(out=result[:], in_=result[:], func=ACT.Tanh)
             nc.sync.dma_start(out=out[rows, cols], in_=result[:])
 
-        def turn_x(i):
-            turn("x", i, on_vector if i % 3 == 0 else on_scalar)
+        def keep_warm(times):
+            idle = sums.tile([P, N_TILE], F32, tag="acc")
+            for n in range(times):
+                nc.tensor.matmul(
+                    out=idle[:], lhsT=ones[:, 0:P], rhs=ones[:], start=True, stop=True
+                )
 
-        turn_x(0)
+        keep_warm(5)
+        def x_copy(i):
+            return on_vector if i == 0 or (i > 2 and i % 2 == 1) else on_scalar
+
+        turn("x", 0, x_copy(0))
         for j in range(ROW_TILES):
             turn("w1", j, on_scalar)
             if j == 0:
                 pack("x", 0)
             else:
                 pack("w1", j - 1)
-            if j == ROW_TILES // 2:
-                b1_all = spread_bias(b1_rows)
-        turn_x(1)
+            if j == 1:
+                keep_warm(1)
+            if j == 3:
+                spread_bias(b1_all, b1_rows, 0)
+            if j == 4:
+                spread_bias(b1_all, b1_rows, 1)
+            if j == 6:
+                spread_bias(b2_all, b2_rows, 0)
+            if j == 7:
+                spread_bias(b2_all, b2_rows, 1)
+        first_layer(0, 0)
+        add_b1(0, 0)
+        turn("x", 1, x_copy(1))
         pack("w1", ROW_TILES - 1)
-        turn_x(2)
+        turn("x", 2, x_copy(2))
         pack("x", 1)
         turn("w2", 0, on_scalar)
         pack("x", 2)
-        turn_x(3)
+        turn("x", 3, x_copy(3))
         pack("w2", 0)
 
         for i in range(ROW_TILES):
+            new_x = i + 3 if 0 < i and i + 3 < ROW_TILES else None
             if i + 1 < ROW_TILES:
                 lift("w2", i + 1)
-            new_x = i + 3 if 0 < i and i + 3 < ROW_TILES else None
             if new_x:
                 lift("x", new_x)
-            for half in range(HALVES):
+            halves = range(HALVES) if i > 0 else range(1, HALVES)
+            for half in halves:
                 first_layer(i, half)
-            if i >= 3:
-                hidden(i - 3)
+            if i >= 2:
+                norm(i - 2)
             if i + 1 < ROW_TILES:
                 settle("w2", i + 1, on_scalar)
-            if new_x and new_x % 3 != 0:
-                settle("x", new_x, on_scalar)
-            if i > 0:
-                norm(i - 1)
-            if 0 < i and i + 2 < ROW_TILES:
-                pack("x", i + 2)
-            if new_x and new_x % 3 == 0:
-                settle("x", new_x, on_vector)
+            if i >= 3:
+                hidden(i - 3)
+            if new_x:
+                settle("x", new_x, x_copy(new_x))
             if i > 0:
                 pack("w2", i)
-            for half in range(HALVES):
+            if 0 < i and i + 2 < ROW_TILES:
+                pack("x", i + 2)
+            for half in halves:
                 add_b1(i, half)
-            if i == 3:
-                b2_all = spread_bias(b2_rows)
             if i >= 4:
                 turn("t", i - 4, on_vector)
             if i >= 5:
                 pack("t", i - 5)
+        norm(ROW_TILES - 2)
         norm(ROW_TILES - 1)
 
         for i in range(ROW_TILES):
-            if i + 5 < ROW_TILES:
-                hidden(i + 5)
+            if 0 < i and i + 4 < ROW_TILES:
+                hidden(i + 4)
             for half in range(HALVES):
                 second_layer(i, half)
             add_b2(i, 0)
-            if 0 < i and i + 3 < ROW_TILES:
-                turn("t", i + 3, on_vector)
             if 0 < i and i + 2 < ROW_TILES:
                 pack("t", i + 2)
+            if 0 < i and i + 3 < ROW_TILES:
+                turn("t", i + 3, on_vector)
             add_b2(i, 1)
-            for half in range(HALVES):
-                finish(i, half)
+            if i > 0:
+                for half in range(HALVES):
+                    finish(i - 1, half)
+        for half in range(HALVES):
+            finish(ROW_TILES - 1, half)

@@ -80,14 +80,14 @@ def tile_modelgraphpolicy_pa_kernel(
                 load_xu(i + 2)
             load_weight(w2_raw, up_w2_self, i)
 
-        x_codes = keep.tile([P, PASSES, BATCH], U32, align_bytes=64)
-        x_scales = keep.tile([P, PASSES, BATCH], U8, align_bytes=64)
+        x_codes = keep.tile([P, ROW_TILES, PASSES * P], U32, align_bytes=64)
+        x_scales = keep.tile([P, ROW_TILES, PASSES * P], U8, align_bytes=64)
         w1_codes = keep.tile([P, PASSES, HID], U32, align_bytes=64)
         w1_scales = keep.tile([P, PASSES, HID], U8, align_bytes=64)
         w2_codes = keep.tile([P, PASSES, HID], U32, align_bytes=64)
         w2_scales = keep.tile([P, PASSES, HID], U8, align_bytes=64)
-        t_codes = keep.tile([P, PASSES, BATCH], U32, align_bytes=64)
-        t_scales = keep.tile([P, PASSES, BATCH], U8, align_bytes=64)
+        t_codes = keep.tile([P, ROW_TILES, PASSES * P], U32, align_bytes=64)
+        t_scales = keep.tile([P, ROW_TILES, PASSES * P], U8, align_bytes=64)
 
         def flip(raw, i):
             words = raw[:].bitcast(F32)
@@ -99,32 +99,18 @@ def tile_modelgraphpolicy_pa_kernel(
                 )
             return bank
 
-        def regroup(copy, bank):
-            grouped = stage.tile([P, PASSES * K_PASS], BF16, align_bytes=64, tag="grouped", bufs=8)
-            copy(
-                out=grouped[:].bitcast(F32).rearrange("p (g r u) -> p g r u", g=PASSES, u=2),
-                in_=bank[:].rearrange("p (g u) r -> p g r u", g=PASSES),
-            )
-            return grouped
-
-        def quantise(grouped, codes, scales, tile_index):
-            cols = slice(tile_index * P, (tile_index + 1) * P)
-            for g in range(PASSES):
-                nc.vector.quantize_mx(
-                    out=codes[:, g, cols].bitcast(FP8X4),
-                    scales=scales[:, g, cols],
-                    in_=grouped[:, g * K_PASS : (g + 1) * K_PASS],
-                )
+        def regroup(copy, bank, words):
+            copy(out=words, in_=bank[:].rearrange("p (g u) r -> p g r u", g=PASSES))
 
         def mx_product(a_codes, a_scales, tile_index, w_codes, w_scales, half):
             acc = sums.tile([P, N_TILE], F32, tag="acc")
-            rows = slice(tile_index * P, (tile_index + 1) * P)
             cols = slice(half * N_TILE, (half + 1) * N_TILE)
             for g in range(PASSES):
+                rows = slice(g * P, (g + 1) * P)
                 nc.tensor.matmul_mx(
                     out=acc[:],
-                    lhsT=a_codes[:, g, rows].bitcast(FP8X4),
-                    lhsT_scale=a_scales[:, g, rows],
+                    lhsT=a_codes[:, tile_index, rows].bitcast(FP8X4),
+                    lhsT_scale=a_scales[:, tile_index, rows],
                     rhs=w_codes[:, g, cols].bitcast(FP8X4),
                     rhs_scale=w_scales[:, g, cols],
                     start=(g == 0),
@@ -147,21 +133,45 @@ def tile_modelgraphpolicy_pa_kernel(
         codes = {"x": x_codes, "w1": w1_codes, "w2": w2_codes, "t": t_codes}
         scales = {"x": x_scales, "w1": w1_scales, "w2": w2_scales, "t": t_scales}
         grouped = {}
-
         banks = {}
 
         def lift(operand, i):
             banks[operand, i] = flip(raws[operand], i)
 
         def settle(operand, i, copy):
-            grouped[operand, i] = regroup(copy, banks[operand, i])
+            if operand in ("x", "t"):
+                single = stage.tile([P, PASSES * K_PASS], BF16, align_bytes=64, tag="single", bufs=6)
+                grouped[operand, i] = single
+                words = single[:].bitcast(F32).rearrange("p (g r u) -> p g r u", g=PASSES, u=2)
+            else:
+                if i % 2 == 0:
+                    double = stage.tile(
+                        [P, PASSES * 2 * K_PASS], BF16, align_bytes=64, tag="double", bufs=4
+                    )
+                    grouped[operand, i // 2] = double
+                both = grouped[operand, i // 2][:].bitcast(F32)
+                words = both.rearrange("p (g j r u) -> p g j r u", g=PASSES, j=2, u=2)[:, :, i % 2]
+            regroup(copy, banks[operand, i], words)
 
         def turn(operand, i, copy):
             lift(operand, i)
             settle(operand, i, copy)
 
         def pack(operand, i):
-            quantise(grouped[operand, i], codes[operand], scales[operand], i)
+            if operand in ("x", "t"):
+                nc.vector.quantize_mx(
+                    out=codes[operand][:, i, :].bitcast(FP8X4),
+                    scales=scales[operand][:, i, :],
+                    in_=grouped[operand, i][:],
+                )
+            elif i % 2 == 1:
+                cols = slice((i - 1) * P, (i + 1) * P)
+                for g in range(PASSES):
+                    nc.vector.quantize_mx(
+                        out=codes[operand][:, g, cols].bitcast(FP8X4),
+                        scales=scales[operand][:, g, cols],
+                        in_=grouped[operand, i // 2][:, g * 2 * K_PASS : (g + 1) * 2 * K_PASS],
+                    )
 
         b1_all = keep.tile([P, HID], BF16)
         b2_all = keep.tile([P, HID], BF16)
@@ -217,12 +227,14 @@ def tile_modelgraphpolicy_pa_kernel(
                 out=result[:], in0=second[i, half][:], in1=b2_all[:, cols], op=ALU.add
             )
 
-        def finish(i, half):
+        def finish(i, half, pieces=1):
             rows = slice(i * P, (i + 1) * P)
-            cols = slice(half * N_TILE, (half + 1) * N_TILE)
-            result = results[i, half]
-            nc.scalar.activation(out=result[:], in_=result[:], func=ACT.Tanh)
-            nc.sync.dma_start(out=out[rows, cols], in_=result[:])
+            width = N_TILE // pieces
+            for n in range(pieces):
+                piece = results[i, half][:, n * width : (n + 1) * width]
+                cols = slice(half * N_TILE + n * width, half * N_TILE + (n + 1) * width)
+                nc.scalar.activation(out=piece, in_=piece, func=ACT.Tanh)
+                nc.sync.dma_start(out=out[rows, cols], in_=piece)
 
         def keep_warm(times):
             idle = sums.tile([P, N_TILE], F32, tag="acc")
@@ -244,9 +256,9 @@ def tile_modelgraphpolicy_pa_kernel(
                 pack("w1", j - 1)
             if j == 1:
                 keep_warm(1)
-            if j == 3:
+            if j == 2:
                 spread_bias(b1_all, b1_rows, 0)
-            if j == 4:
+            if j == 3:
                 spread_bias(b1_all, b1_rows, 1)
             if j == 6:
                 spread_bias(b2_all, b2_rows, 0)
@@ -265,25 +277,25 @@ def tile_modelgraphpolicy_pa_kernel(
 
         for i in range(ROW_TILES):
             new_x = i + 3 if 0 < i and i + 3 < ROW_TILES else None
-            if i + 1 < ROW_TILES:
-                lift("w2", i + 1)
             if new_x:
                 lift("x", new_x)
+            if i + 1 < ROW_TILES:
+                lift("w2", i + 1)
             halves = range(HALVES) if i > 0 else range(1, HALVES)
             for half in halves:
                 first_layer(i, half)
             if i >= 2:
                 norm(i - 2)
-            if i + 1 < ROW_TILES:
-                settle("w2", i + 1, on_scalar)
             if i >= 3:
                 hidden(i - 3)
             if new_x:
                 settle("x", new_x, x_copy(new_x))
-            if i > 0:
-                pack("w2", i)
+            if i + 1 < ROW_TILES:
+                settle("w2", i + 1, on_vector if i + 1 == ROW_TILES - 1 else on_scalar)
             if 0 < i and i + 2 < ROW_TILES:
                 pack("x", i + 2)
+            if i > 0:
+                pack("w2", i)
             for half in halves:
                 add_b1(i, half)
             if i >= 4:
@@ -294,18 +306,15 @@ def tile_modelgraphpolicy_pa_kernel(
         norm(ROW_TILES - 1)
 
         for i in range(ROW_TILES):
-            if 0 < i and i + 4 < ROW_TILES:
-                hidden(i + 4)
+            if i + 5 < ROW_TILES:
+                hidden(i + 5)
             for half in range(HALVES):
                 second_layer(i, half)
+            if 1 < i and i + 1 < ROW_TILES:
+                pack("t", i + 1)
             add_b2(i, 0)
-            if 0 < i and i + 2 < ROW_TILES:
-                pack("t", i + 2)
-            if 0 < i and i + 3 < ROW_TILES:
-                turn("t", i + 3, on_vector)
+            if 1 < i and i + 2 < ROW_TILES:
+                turn("t", i + 2, on_vector)
             add_b2(i, 1)
-            if i > 0:
-                for half in range(HALVES):
-                    finish(i - 1, half)
-        for half in range(HALVES):
-            finish(ROW_TILES - 1, half)
+            finish(i, 0)
+            finish(i, 1, pieces=2 if i == ROW_TILES - 1 else 1)

from contextlib import ExitStack

import concourse.mybir as mybir
from concourse.masks import make_identity

F32 = mybir.dt.float32
BF16 = mybir.dt.bfloat16
U32 = mybir.dt.uint32
U8 = mybir.dt.uint8
FP8X4 = mybir.dt.float8_e4m3fn_x4
ALU = mybir.AluOpType
ACT = mybir.ActivationFunctionType

P = 128
PACK = 4
K_PASS = P * PACK
BATCH = 1024
STATE = 896
FEAT = 1024
HID = 1024
PASSES = FEAT // K_PASS
N_TILE = 512
HALVES = HID // N_TILE
ROW_TILES = BATCH // P
WORDS = FEAT // 2
EPS = 1e-12

FLOPS = 2 * BATCH * FEAT * HID + 2 * BATCH * HID * HID


def tile_modelgraphpolicy_pa_kernel(
    tc, state, action, up_w1, up_b1, up_w2_self, up_b2, out
):
    nc = tc.nc
    with ExitStack() as ctx:
        keep = ctx.enter_context(tc.tile_pool(name="keep", bufs=1))
        stage = ctx.enter_context(tc.tile_pool(name="stage", bufs=2))
        flipped = ctx.enter_context(tc.psum_pool(name="flipped", bufs=4))
        sums = ctx.enter_context(tc.psum_pool(name="sums", bufs=4))
        ctx.enter_context(tc.manual_schedule())

        ident = keep.tile([P, P], F32)
        make_identity(nc, ident[:])
        ones = keep.tile([P, N_TILE], BF16)
        nc.gpsimd.memset(ones[:], 1.0)
        neg_half = keep.tile([P, 1], F32)
        nc.gpsimd.memset(neg_half[:], -0.5)
        b1_rows = keep.tile([P, HID], BF16)
        nc.vector.memset(b1_rows[:].bitcast(U32), 0)
        b2_rows = keep.tile([P, HID], BF16)
        nc.vector.memset(b2_rows[:].bitcast(U32), 0)

        nc.scalar.dma_start(
            out=b1_rows[0:1, :], in_=up_b1.rearrange("(o h) -> o h", o=1)
        )
        nc.scalar.dma_start(out=b2_rows[0:1, :], in_=up_b2.rearrange("(o h) -> o h", o=1))
        warm = keep.tile([P, 1], F32)
        nc.scalar.activation(out=warm[:], in_=neg_half[:], func=ACT.Tanh)

        x_raw = keep.tile([P, ROW_TILES * FEAT], BF16)
        w1_raw = keep.tile([P, ROW_TILES * FEAT], BF16)
        w2_raw = keep.tile([P, ROW_TILES * FEAT], BF16)

        def load_xu(i):
            rows = slice(i * P, (i + 1) * P)
            nc.sync.dma_start(out=x_raw[:, i * FEAT : i * FEAT + STATE], in_=state[rows, :])
            nc.sync.dma_start(out=x_raw[:, i * FEAT + STATE : (i + 1) * FEAT], in_=action[rows, :])

        def load_weight(raw, weight, j):
            nc.sync.dma_start(
                out=raw[:, j * FEAT : (j + 1) * FEAT], in_=weight[j * P : (j + 1) * P, :]
            )

        load_xu(0)
        for j in range(ROW_TILES):
            load_weight(w1_raw, up_w1, j)
        load_xu(1)
        for i in range(ROW_TILES):
            if i + 2 < ROW_TILES:
                load_xu(i + 2)
            load_weight(w2_raw, up_w2_self, i)

        x_codes = keep.tile([P, ROW_TILES, PASSES * P], U32, align_bytes=64)
        x_scales = keep.tile([P, ROW_TILES, PASSES * P], U8, align_bytes=64)
        w1_codes = keep.tile([P, PASSES, HID], U32, align_bytes=64)
        w1_scales = keep.tile([P, PASSES, HID], U8, align_bytes=64)
        w2_codes = keep.tile([P, PASSES, HID], U32, align_bytes=64)
        w2_scales = keep.tile([P, PASSES, HID], U8, align_bytes=64)
        t_codes = keep.tile([P, ROW_TILES, PASSES * P], U32, align_bytes=64)
        t_scales = keep.tile([P, ROW_TILES, PASSES * P], U8, align_bytes=64)

        def flip(raw, i):
            words = raw[:].bitcast(F32)
            bank = flipped.tile([P, PACK, P], F32, tag="bank")
            for s in range(PACK):
                first = i * WORDS + s * P
                nc.tensor.transpose(
                    out=bank[:, s, :], in_=words[:, first : first + P], identity=ident[:]
                )
            return bank

        def regroup(copy, bank, words):
            copy(out=words, in_=bank[:].rearrange("p (g u) r -> p g r u", g=PASSES))

        def mx_product(a_codes, a_scales, tile_index, w_codes, w_scales, half):
            acc = sums.tile([P, N_TILE], F32, tag="acc")
            cols = slice(half * N_TILE, (half + 1) * N_TILE)
            for g in range(PASSES):
                rows = slice(g * P, (g + 1) * P)
                nc.tensor.matmul_mx(
                    out=acc[:],
                    lhsT=a_codes[:, tile_index, rows].bitcast(FP8X4),
                    lhsT_scale=a_scales[:, tile_index, rows],
                    rhs=w_codes[:, g, cols].bitcast(FP8X4),
                    rhs_scale=w_scales[:, g, cols],
                    start=(g == 0),
                    stop=(g == PASSES - 1),
                )
            return acc

        def spread_bias(everywhere, rows, half):
            cols = slice(half * N_TILE, (half + 1) * N_TILE)
            spread = sums.tile([P, N_TILE], BF16, tag="acc")
            nc.tensor.matmul(out=spread[:], lhsT=ones[:, 0:P], rhs=rows[:, cols], start=True, stop=True)
            nc.vector.tensor_copy(out=everywhere[:, cols], in_=spread[:])

        z_all = keep.tile([P, ROW_TILES, HID], F32)
        t_all = keep.tile([P, ROW_TILES * HID], BF16)
        sum_sq = keep.tile([P, ROW_TILES], F32)
        floored = keep.tile([P, ROW_TILES], F32)
        inv_norm = keep.tile([P, ROW_TILES], F32)
        raws = {"x": x_raw, "w1": w1_raw, "w2": w2_raw, "t": t_all}
        codes = {"x": x_codes, "w1": w1_codes, "w2": w2_codes, "t": t_codes}
        scales = {"x": x_scales, "w1": w1_scales, "w2": w2_scales, "t": t_scales}
        grouped = {}
        banks = {}

        def lift(operand, i):
            banks[operand, i] = flip(raws[operand], i)

        def settle(operand, i, copy):
            if operand in ("x", "t"):
                single = stage.tile([P, PASSES * K_PASS], BF16, align_bytes=64, tag="single", bufs=6)
                grouped[operand, i] = single
                words = single[:].bitcast(F32).rearrange("p (g r u) -> p g r u", g=PASSES, u=2)
            else:
                if i % 2 == 0:
                    double = stage.tile(
                        [P, PASSES * 2 * K_PASS], BF16, align_bytes=64, tag="double", bufs=4
                    )
                    grouped[operand, i // 2] = double
                both = grouped[operand, i // 2][:].bitcast(F32)
                words = both.rearrange("p (g j r u) -> p g j r u", g=PASSES, j=2, u=2)[:, :, i % 2]
            regroup(copy, banks[operand, i], words)

        def turn(operand, i, copy):
            lift(operand, i)
            settle(operand, i, copy)

        def pack(operand, i):
            if operand in ("x", "t"):
                nc.vector.quantize_mx(
                    out=codes[operand][:, i, :].bitcast(FP8X4),
                    scales=scales[operand][:, i, :],
                    in_=grouped[operand, i][:],
                )
            elif i % 2 == 1:
                cols = slice((i - 1) * P, (i + 1) * P)
                for g in range(PASSES):
                    nc.vector.quantize_mx(
                        out=codes[operand][:, g, cols].bitcast(FP8X4),
                        scales=scales[operand][:, g, cols],
                        in_=grouped[operand, i // 2][:, g * 2 * K_PASS : (g + 1) * 2 * K_PASS],
                    )

        b1_all = keep.tile([P, HID], BF16)
        b2_all = keep.tile([P, HID], BF16)

        on_scalar = nc.scalar.copy
        on_vector = nc.vector.tensor_copy
        first = {}
        second = {}

        def first_layer(i, half):
            first[i, half] = mx_product(x_codes, x_scales, i, w1_codes, w1_scales, half)

        def add_b1(i, half):
            cols = slice(half * N_TILE, (half + 1) * N_TILE)
            nc.vector.tensor_tensor(
                out=z_all[:, i, cols], in0=first[i, half][:], in1=b1_all[:, cols], op=ALU.add
            )

        def norm(i):
            squares = stage.tile([P, HID], BF16, tag="squares")
            nc.scalar.activation(
                out=squares[:], in_=z_all[:, i, :], func=ACT.Square, accum_out=sum_sq[:, i : i + 1]
            )
            nc.gpsimd.tensor_scalar(
                out=floored[:, i : i + 1],
                in0=sum_sq[:, i : i + 1],
                scalar1=EPS * EPS,
                scalar2=None,
                op0=ALU.max,
            )
            nc.gpsimd.tensor_tensor(
                out=inv_norm[:, i : i + 1], in0=floored[:, i : i + 1], in1=neg_half[:], op=ALU.pow
            )

        def hidden(i):
            nc.scalar.activation(
                out=t_all[:, i * HID : (i + 1) * HID],
                in_=z_all[:, i, :],
                func=ACT.Tanh,
                scale=inv_norm[:, i : i + 1],
            )

        def second_layer(i, half):
            second[i, half] = mx_product(t_codes, t_scales, i, w2_codes, w2_scales, half)

        results = {}

        def add_b2(i, half):
            cols = slice(half * N_TILE, (half + 1) * N_TILE)
            result = stage.tile([P, N_TILE], F32, tag="result", bufs=8)
            results[i, half] = result
            nc.vector.tensor_tensor(
                out=result[:], in0=second[i, half][:], in1=b2_all[:, cols], op=ALU.add
            )

        def finish(i, half, pieces=1):
            rows = slice(i * P, (i + 1) * P)
            width = N_TILE // pieces
            for n in range(pieces):
                piece = results[i, half][:, n * width : (n + 1) * width]
                cols = slice(half * N_TILE + n * width, half * N_TILE + (n + 1) * width)
                nc.scalar.activation(out=piece, in_=piece, func=ACT.Tanh)
                nc.sync.dma_start(out=out[rows, cols], in_=piece)

        def keep_warm(times):
            idle = sums.tile([P, N_TILE], F32, tag="acc")
            for n in range(times):
                nc.tensor.matmul(
                    out=idle[:], lhsT=ones[:, 0:P], rhs=ones[:], start=True, stop=True
                )

        keep_warm(5)
        def x_copy(i):
            return on_vector if i == 0 or (i > 2 and i % 2 == 1) else on_scalar

        turn("x", 0, x_copy(0))
        for j in range(ROW_TILES):
            turn("w1", j, on_scalar)
            if j == 0:
                pack("x", 0)
            else:
                pack("w1", j - 1)
            if j == 1:
                keep_warm(1)
            if j == 2:
                spread_bias(b1_all, b1_rows, 0)
            if j == 3:
                spread_bias(b1_all, b1_rows, 1)
            if j == 6:
                spread_bias(b2_all, b2_rows, 0)
            if j == 7:
                spread_bias(b2_all, b2_rows, 1)
        first_layer(0, 0)
        add_b1(0, 0)
        turn("x", 1, x_copy(1))
        pack("w1", ROW_TILES - 1)
        turn("x", 2, x_copy(2))
        pack("x", 1)
        turn("w2", 0, on_scalar)
        pack("x", 2)
        turn("x", 3, x_copy(3))
        pack("w2", 0)

        for i in range(ROW_TILES):
            new_x = i + 3 if 0 < i and i + 3 < ROW_TILES else None
            if new_x:
                lift("x", new_x)
            if i + 1 < ROW_TILES:
                lift("w2", i + 1)
            halves = range(HALVES) if i > 0 else range(1, HALVES)
            for half in halves:
                first_layer(i, half)
            if i >= 2:
                norm(i - 2)
            if i >= 3:
                hidden(i - 3)
            if new_x:
                settle("x", new_x, x_copy(new_x))
            if i + 1 < ROW_TILES:
                settle("w2", i + 1, on_vector if i + 1 == ROW_TILES - 1 else on_scalar)
            if 0 < i and i + 2 < ROW_TILES:
                pack("x", i + 2)
            if i > 0:
                pack("w2", i)
            for half in halves:
                add_b1(i, half)
            if i >= 4:
                turn("t", i - 4, on_vector)
            if i >= 5:
                pack("t", i - 5)
        norm(ROW_TILES - 2)
        norm(ROW_TILES - 1)

        for i in range(ROW_TILES):
            if i + 5 < ROW_TILES:
                hidden(i + 5)
            for half in range(HALVES):
                second_layer(i, half)
            if 1 < i and i + 1 < ROW_TILES:
                pack("t", i + 1)
            add_b2(i, 0)
            if 1 < i and i + 2 < ROW_TILES:
                turn("t", i + 2, on_vector)
            add_b2(i, 1)
            finish(i, 0)
            finish(i, 1, pieces=2 if i == ROW_TILES - 1 else 1)
